import numpy as np
import ml_dtypes


def mxq(x, axis, fmt="e4m3"):
    dtype, down = {"e4m3": (ml_dtypes.float8_e4m3fn, 7), "e5m2": (ml_dtypes.float8_e5m2, 14)}[fmt]
    v = np.moveaxis(np.asarray(x, np.float32).astype(ml_dtypes.bfloat16).astype(np.float64), axis, -1)
    blocks = v.reshape(v.shape[:-1] + (-1, 32))
    amax = np.abs(blocks).max(-1, keepdims=True)
    byte = np.maximum(np.where(amax > 0, np.frexp(amax)[1] - 1 + 127, 0) - down, 1)
    scale = np.exp2(byte - 127.0)
    codes = (blocks / scale).astype(np.float32).astype(dtype).astype(np.float64)
    return np.moveaxis((codes * scale).reshape(v.shape), -1, axis)


WIDE = False


def mx_kscale(k):
    if not WIDE:
        return np.ones(k)
    levels = np.array([10, -10, 5, -5, 0])
    a = np.random.permutation(np.resize(levels, k // 512 * 4)).reshape(k // 512, 4)
    idx = np.arange(k)
    return np.exp2(a[idx // 512, idx % 128 // 32])


BF16 = ml_dtypes.bfloat16


def bf(x):
    return np.asarray(x, np.float32).astype(BF16)


def f64(x):
    return np.asarray(x).astype(np.float64)


E2M1 = np.array([0.0, 0.5, 1.0, 1.5, 2.0, 3.0, 4.0, 6.0, -0.0, -0.5, -1.0, -1.5, -2.0, -3.0, -4.0, -6.0])


def pack_weight(w, fmt):
    k, n = w.shape
    w = f64(bf(w)).reshape(k // 32, 32, n)
    amax = np.abs(w).max(1)
    if fmt == "e4m3":
        byte = np.frexp(amax)[1] - 1 + 127 - 7
    else:
        mant, ex = np.frexp(amax / 6.0)
        byte = np.where(mant > 0.5, ex, ex - 1) + 127
    byte = np.clip(np.where(amax > 0, byte, 1), 1, 254)
    scaled = (w * np.exp2(127.0 - byte)[:, None, :]).reshape(k, n).astype(np.float32)
    by_word = np.ascontiguousarray(scaled.reshape(k // 512, 128, 4, n).transpose(0, 1, 3, 2))
    if fmt == "e4m3":
        words = by_word.astype(ml_dtypes.float8_e4m3fn).view(np.uint8)
    else:
        c = by_word.astype(ml_dtypes.float4_e2m1fn).view(np.uint8) & 0xF
        words = c[..., 0::2] | (c[..., 1::2] << 4)
    return np.ascontiguousarray(words), np.ascontiguousarray(byte.astype(np.uint8).reshape(k // 512, 16, n))


def unpack_weight(words, scales, fmt):
    g, p, n, _ = words.shape
    if fmt == "e4m3":
        vals = np.ascontiguousarray(words).view(ml_dtypes.float8_e4m3fn).astype(np.float64)
    else:
        nib = np.empty((g, p, n, 4), np.uint8)
        nib[..., 0::2] = words & 0xF
        nib[..., 1::2] = words >> 4
        vals = E2M1[nib]
    vals = vals * np.repeat(np.exp2(scales.astype(np.float64) - 127.0), 8, axis=1)[..., None]
    return vals.transpose(0, 1, 3, 2).reshape(g * 512, n)


B, H0, W0, H1, W1, C = 1, 8, 16, 8, 16, 4096
L, S = H0 * W0, H1 * W1
THR = 0.2
TEMPERATURE = 0.1
BORDER = 2
NM = min(L, S) // 2
ND = NM // 16
DUP = 0.92
RB = 0.5
ZT = 4.5
SD = ZT - np.sqrt(ZT**2 - 2.0 * np.log(min(L, S) * THR / (1.0 - THR)))
SIG = SD / np.sqrt(1.0 + RB**2 / 2.0)
G = np.sqrt(SIG * TEMPERATURE * np.sqrt(C / 2.0))
MATCH = np.log(max(L, S)) + SD**2 / 2.0 + 3.5
ALPHA = MATCH / (SIG * np.sqrt(C / 2.0))


def interior_mask(h, w, b):
    vh = (np.arange(h) >= b) & (np.arange(h) < h - b)
    vw = (np.arange(w) >= b) & (np.arange(w) < w - b)
    return (vh[:, None] & vw[None, :]).reshape(-1)


def softmax(v, axis):
    e = np.exp(v - v.max(axis=axis, keepdims=True))
    return e / e.sum(axis=axis, keepdims=True)


def pick(h, w):
    rep = np.random.permutation(np.flatnonzero(interior_mask(h, w, BORDER)))[:ND]
    rest = np.random.permutation(np.setdiff1d(np.arange(h * w), rep))[:NM]
    return rep, rest


def setup_inputs():
    s = mx_kscale(C)
    x0 = np.random.standard_normal((B, L, C))
    x1 = np.random.standard_normal((B, S, C))
    for n in range(B):
        r0, m0 = pick(H0, W0)
        r1, m1 = pick(H1, W1)
        x1[n, m1] = ALPHA * x0[n, m0] + np.sqrt(1.0 - ALPHA**2) * x1[n, m1]
        x0[n, r0] = DUP * x0[n, m0[:ND]]
        x1[n, r1] = DUP * x1[n, m1[:ND]]
    w = np.random.standard_normal((C, C)) * G / np.sqrt(C) / s[None, :]
    words, scales = pack_weight(np.ascontiguousarray(w.T), "e4m3")
    return {"feat_c0": bf(x0 * s),
            "feat_c1": bf(x1 * s),
            "W_words": words,
            "W_scales": scales,
            "b": bf(np.random.standard_normal(C) * RB * G),
            "h0c": H0, "w0c": W0, "h1c": H1, "w1c": W1}


def reference(feat_c0, feat_c1, W_words, W_scales, b, h0c, w0c, h1c, w1c):
    scale = feat_c0.shape[-1] ** 0.5
    wt = unpack_weight(W_words, W_scales, "e4m3")
    f0 = ((mxq(f64(feat_c0), 2, "e4m3") @ wt) + f64(b)) / scale
    f1 = ((mxq(f64(feat_c1), 2, "e4m3") @ wt) + f64(b)) / scale
    sim = (mxq(f0, 2, "e4m3") @ mxq(f1, 2, "e4m3").transpose(0, 2, 1)) / TEMPERATURE

    conf_0to1 = softmax(sim, 2)
    conf_1to0 = softmax(sim, 1)

    mask = (conf_0to1 > THR) & (conf_0to1 == conf_0to1.max(axis=2, keepdims=True))
    mask = mask | ((conf_1to0 > THR) & (conf_1to0 == conf_1to0.max(axis=1, keepdims=True)))

    mask = mask & interior_mask(h0c, w0c, BORDER)[None, :, None]
    mask = mask & interior_mask(h1c, w1c, BORDER)[None, None, :]

    mconf = np.where(mask, np.maximum(conf_0to1, conf_1to0), 0.0)
    return np.stack([conf_0to1, conf_1to0, mconf])

@@ -1,0 +1,242 @@
+from contextlib import ExitStack
+
+import concourse.mybir as mybir
+from concourse.masks import make_identity
+
+F32 = mybir.dt.float32
+BF16 = mybir.dt.bfloat16
+I32 = mybir.dt.int32
+U32 = mybir.dt.uint32
+U8 = mybir.dt.uint8
+FP8X4 = mybir.dt.float8_e4m3fn_x4
+ALU = mybir.AluOpType
+ACT = mybir.ActivationFunctionType
+AX = mybir.AxisListType
+
+P = 128
+C = 4096
+GROUPS = C // 512
+CHUNK = 1024
+NCHUNK = C // CHUNK
+TILES = CHUNK // P
+TOK = 2 * P
+THR = 0.2
+INV_T = 10.0
+BORDER = 2
+MANUAL = False
+
+FLOPS = 2 * TOK * C * C + 2 * P * P * C
+
+
+def tile_coarsematching_w_kernel(tc, feat_c0, feat_c1, W_words, W_scales, b, h0c, w0c, h1c, w1c, out):
+    nc = tc.nc
+    feats = (feat_c0[0], feat_c1[0])
+    with ExitStack() as ctx:
+        keep = ctx.enter_context(tc.tile_pool(name="keep", bufs=1))
+        xgp = ctx.enter_context(tc.tile_pool(name="xgp", bufs=4))
+        ftp = ctx.enter_context(tc.tile_pool(name="ftp", bufs=2))
+        fgp = ctx.enter_context(tc.tile_pool(name="fgp", bufs=3))
+        psum = ctx.enter_context(tc.psum_pool(name="psum", bufs=1))
+        if MANUAL:
+            ctx.enter_context(tc.manual_schedule())
+
+        dummy = keep.tile([P, 1], F32, name="dummy")
+        nc.vector.memset(dummy[:], 0.0)
+        dummy2 = keep.tile([P, 1], F32, name="dummy2")
+        nc.scalar.activation(out=dummy2[:], in_=dummy[:], func=ACT.Exp)
+        brow = keep.tile([P, P], BF16, name="brow")
+        nc.vector.memset(brow[:], 0.0)
+        planes = keep.tile([P, 2, C], U8, name="planes", align_bytes=64)
+        for a in range(2):
+            nc.vector.memset(planes[:, a, :].bitcast(I32), 0)
+        ident = keep.tile([P, P], F32, name="ident")
+        make_identity(nc, ident[:])
+
+        xraw = []
+        for h in range(2):
+            pair = []
+            for s in range(2):
+                xr = keep.tile([P, C // 2], BF16, name="xraw%d_%d" % (h, s))
+                nc.sync.dma_start(out=xr[:], in_=feats[s][:, (C // 2) * h : (C // 2) * (h + 1)])
+                pair.append(xr)
+            xraw.append(pair)
+        nc.scalar.dma_start(out=brow[0 : C // P, :], in_=b.rearrange("(j p) -> j p", p=P))
+        for a in range(2):
+            for q in range(4):
+                nc.sync.dma_start(
+                    out=planes[32 * q : 32 * q + 16, a, :].bitcast(I32),
+                    in_=W_scales[4 * a : 4 * a + 4, 4 * q : 4 * q + 4, :].bitcast(I32),
+                )
+        wt = []
+        for c in range(NCHUNK):
+            row = []
+            for g in range(GROUPS):
+                w = keep.tile([P, CHUNK], U32, name="w%d_%d" % (c, g), align_bytes=64)
+                nc.sync.dma_start(
+                    out=w[:].bitcast(I32),
+                    in_=W_words[g].rearrange("p n t -> p (n t)")[:, 4 * CHUNK * c : 4 * CHUNK * (c + 1)].bitcast(I32),
+                )
+                row.append(w)
+            wt.append(row)
+
+        rows = []
+        for i, (h, w) in enumerate(((h0c, w0c), (h1c, w1c))):
+            r = keep.tile([P, P], F32, name="rowmask%d" % i)
+            nc.vector.memset(r[:], 0.0)
+            nc.vector.memset(r[:].rearrange("p (r c) -> p r c", c=w)[:, BORDER : h - BORDER, BORDER : w - BORDER], 1.0)
+            rows.append(r)
+        setup_ps = psum.tile([P, 2, P], F32, tag="bank7", name="setup_ps")
+        for i in range(2):
+            nc.tensor.transpose(setup_ps[:, i, :], rows[i][:], ident[:])
+        im = keep.tile([P, P], F32, name="im")
+        nc.vector.tensor_tensor(out=im[:], in0=setup_ps[:, 0, :], in1=rows[1][:], op=ALU.mult)
+        imt = keep.tile([P, P], F32, name="imt")
+        nc.vector.tensor_tensor(out=imt[:], in0=setup_ps[:, 1, :], in1=rows[0][:], op=ALU.mult)
+
+        xcodes = keep.tile([P, GROUPS, TOK], U32, name="xcodes", align_bytes=64)
+        xplanes = keep.tile([P, GROUPS, TOK], U8, name="xplanes", align_bytes=64)
+        xts = []
+        for g in range(GROUPS):
+            xt = psum.tile([P, 2, TOK], F32, tag="bank%d" % g, name="xt%d" % g)
+            for s in range(2):
+                words = xraw[g // 4][s][:].bitcast(F32)
+                for u in range(2):
+                    lo = 256 * (g % 4)
+                    nc.tensor.transpose(xt[:, u, P * s : P * (s + 1)], words[:, lo + u : lo + 256 : 2], ident[:])
+            xts.append(xt)
+        xgs = {}
+
+        def x_copy(g):
+            xg = xgp.tile([P, 4 * TOK], BF16, name="xg", align_bytes=64)
+            dst = xg[:].bitcast(F32).rearrange("p (k u) -> p k u", u=2)
+            src = xts[g][:].rearrange("p u k -> p k u")
+            if g % 2 == 0:
+                nc.vector.tensor_copy(out=dst, in_=src)
+            else:
+                nc.scalar.copy(out=dst, in_=src)
+            xgs[g] = xg
+
+        def x_quant(g):
+            nc.vector.quantize_mx(out=xcodes[:, g, :].bitcast(FP8X4), scales=xplanes[:, g, :], in_=xgs[g][:])
+
+        x_copy(0)
+        x_copy(1)
+        for g in range(GROUPS):
+            if g + 2 < GROUPS:
+                x_copy(g + 2)
+            x_quant(g)
+
+        bq = keep.tile([P, P], F32, name="bq")
+        nc.vector.tensor_scalar_mul(bq[:], brow[:], 1.0 / 64.0)
+        bias_ps = psum.tile([P, P], F32, tag="bank0", name="bias_ps")
+        nc.tensor.transpose(bias_ps[:], bq[:], ident[:])
+        bias_t = keep.tile([P, C // P], F32, name="bias_t")
+        nc.vector.tensor_copy(out=bias_t[:], in_=bias_ps[:, 0 : C // P])
+
+        fcodes = keep.tile([P, GROUPS, TOK], U32, name="fcodes", align_bytes=64)
+        fplanes = keep.tile([P, GROUPS, TOK], U8, name="fplanes", align_bytes=64)
+        for c in range(NCHUNK):
+            accs = []
+            for j in range(TILES):
+                acc = psum.tile([P, TOK], F32, tag="bank%d" % j, name="acc%d_%d" % (c, j))
+                accs.append(acc)
+            for g in range(GROUPS):
+                k = 4 * (g % 4)
+                for j in range(TILES):
+                    nc.tensor.matmul_mx(
+                        out=accs[j][:],
+                        lhsT=wt[c][g][:, P * j : P * (j + 1)].bitcast(FP8X4),
+                        lhsT_scale=planes[k:P, g // 4, CHUNK * c + P * j : CHUNK * c + P * (j + 1)],
+                        rhs=xcodes[:, g, :].bitcast(FP8X4),
+                        rhs_scale=xplanes[:, g, :],
+                        start=(g == 0),
+                        stop=(g == GROUPS - 1),
+                    )
+            ft = ftp.tile([P, TILES, TOK], BF16, name="ft")
+            for j in range(TILES):
+                col = TILES * c + j
+                if j % 2 == 0:
+                    nc.scalar.activation(
+                        out=ft[:, j, :], in_=accs[j][:], func=ACT.Identity, bias=bias_t[:, col : col + 1], scale=1.0 / 64.0
+                    )
+                else:
+                    nc.vector.tensor_scalar(
+                        out=ft[:, j, :], in0=accs[j][:], scalar1=1.0 / 64.0, scalar2=bias_t[:, col : col + 1],
+                        op0=ALU.mult, op1=ALU.add,
+                    )
+            fgs = []
+            for h in range(2):
+                fg = fgp.tile([P, 4 * TOK], BF16, name="fg", align_bytes=64)
+                nc.vector.tensor_copy(
+                    out=fg[:].rearrange("p (c i t) -> p c t i", i=4, t=4),
+                    in_=ft[:, 4 * h : 4 * h + 4, :].rearrange("p t (c i) -> p c t i", i=4),
+                )
+                fgs.append(fg)
+            for h in range(2):
+                nc.vector.quantize_mx(
+                    out=fcodes[:, 2 * c + h, :].bitcast(FP8X4), scales=fplanes[:, 2 * c + h, :], in_=fgs[h][:]
+                )
+
+        sim_t = psum.tile([P, P], F32, tag="bank0", name="sim_t")
+        sim = psum.tile([P, P], F32, tag="bank1", name="sim")
+        sim_t2 = psum.tile([P, P], F32, tag="bank2", name="sim_t2")
+        sim2 = psum.tile([P, P], F32, tag="bank3", name="sim2")
+        for c2 in range(GROUPS):
+            for dst, lo_l, lo_r in ((sim_t, P, 0), (sim, 0, P), (sim_t2, P, 0), (sim2, 0, P)):
+                nc.tensor.matmul_mx(
+                    out=dst[:],
+                    lhsT=fcodes[:, c2, lo_l : lo_l + P].bitcast(FP8X4),
+                    lhsT_scale=fplanes[:, c2, lo_l : lo_l + P],
+                    rhs=fcodes[:, c2, lo_r : lo_r + P].bitcast(FP8X4),
+                    rhs_scale=fplanes[:, c2, lo_r : lo_r + P],
+                    start=(c2 == 0),
+                    stop=(c2 == GROUPS - 1),
+                )
+
+        mx = keep.tile([P, 2], F32, name="mx")
+        nb = keep.tile([P, 2], F32, name="nb")
+        sums = keep.tile([P, 2], F32, name="sums")
+        rec = keep.tile([P, 2], F32, name="rec")
+        e_t = keep.tile([P, P], F32, name="e_t")
+        e_n = keep.tile([P, P], F32, name="e_n")
+        for i, ps in enumerate((sim_t, sim)):
+            nc.vector.reduce_max(out=mx[:, i : i + 1], in_=ps[:], axis=AX.X)
+            nc.vector.tensor_scalar_mul(nb[:, i : i + 1], mx[:, i : i + 1], -INV_T)
+        for i, (ps, e) in enumerate(((sim_t, e_t), (sim, e_n))):
+            nc.scalar.activation(
+                out=e[:], in_=ps[:], func=ACT.Exp, bias=nb[:, i : i + 1], scale=INV_T, accum_out=sums[:, i : i + 1]
+            )
+        g_t = keep.tile([P, P], F32, name="g_t")
+        nc.vector.scalar_tensor_tensor(
+            out=g_t[:], in0=sim_t2[:], scalar=mx[:, 0:1], in1=imt[:], op0=ALU.is_equal, op1=ALU.mult
+        )
+        nc.vector.reciprocal(out=rec[:, 0:1], in_=sums[:, 0:1])
+        c_t = keep.tile([P, P], F32, name="c_t")
+        nc.vector.tensor_scalar_mul(c_t[:], e_t[:], rec[:, 0:1])
+        k_t = keep.tile([P, P], F32, name="k_t")
+        nc.vector.scalar_tensor_tensor(out=k_t[:], in0=c_t[:], scalar=THR, in1=g_t[:], op0=ALU.is_gt, op1=ALU.mult)
+        back1 = psum.tile([P, P], F32, tag="bank4", name="back1")
+        nc.tensor.transpose(back1[:], c_t[:], ident[:])
+        back2 = psum.tile([P, 2, P], F32, tag="bank5", name="back2")
+        nc.tensor.transpose(back2[:, 0, :], c_t[:], ident[:])
+        nc.tensor.transpose(back2[:, 1, :], k_t[:], ident[:])
+        c10 = keep.tile([P, P], F32, name="c10")
+        nc.scalar.copy(out=c10[:], in_=back1[:])
+        nc.sync.dma_start(out=out[1, 0], in_=c10[:])
+
+        g_n = keep.tile([P, P], F32, name="g_n")
+        nc.vector.scalar_tensor_tensor(
+            out=g_n[:], in0=sim2[:], scalar=mx[:, 1:2], in1=im[:], op0=ALU.is_equal, op1=ALU.mult
+        )
+        nc.vector.reciprocal(out=rec[:, 1:2], in_=sums[:, 1:2])
+        own = keep.tile([P, 2, P], F32, name="own")
+        nc.vector.tensor_scalar_mul(own[:, 0, :], e_n[:], rec[:, 1:2])
+        nc.sync.dma_start(out=out[0, 0], in_=own[:, 0, :])
+        nc.vector.scalar_tensor_tensor(
+            out=own[:, 1, :], in0=own[:, 0, :], scalar=THR, in1=g_n[:], op0=ALU.is_gt, op1=ALU.mult
+        )
+        both = keep.tile([P, 2, P], F32, name="both")
+        nc.vector.tensor_tensor(out=both[:], in0=own[:], in1=back2[:], op=ALU.max)
+        mconf = keep.tile([P, P], F32, name="mconf")
+        nc.vector.tensor_tensor(out=mconf[:], in0=both[:, 0, :], in1=both[:, 1, :], op=ALU.mult)
+        nc.sync.dma_start(out=out[2, 0], in_=mconf[:])

@@ -11,19 +11,16 @@ U8 = mybir.dt.uint8
 FP8X4 = mybir.dt.float8_e4m3fn_x4
 ALU = mybir.AluOpType
 ACT = mybir.ActivationFunctionType
-AX = mybir.AxisListType
 
 P = 128
 C = 4096
 GROUPS = C // 512
-CHUNK = 1024
-NCHUNK = C // CHUNK
-TILES = CHUNK // P
 TOK = 2 * P
+BANKS = 8
+CHUNKS = ((0, 4), (4, 8), (12, 8), (20, 8), (28, 4))
 THR = 0.2
 INV_T = 10.0
 BORDER = 2
-MANUAL = False
 
 FLOPS = 2 * TOK * C * C + 2 * P * P * C
 
@@ -31,14 +28,14 @@ FLOPS = 2 * TOK * C * C + 2 * P * P * C
 def tile_coarsematching_w_kernel(tc, feat_c0, feat_c1, W_words, W_scales, b, h0c, w0c, h1c, w1c, out):
     nc = tc.nc
     feats = (feat_c0[0], feat_c1[0])
+    half = C // 2
     with ExitStack() as ctx:
         keep = ctx.enter_context(tc.tile_pool(name="keep", bufs=1))
         xgp = ctx.enter_context(tc.tile_pool(name="xgp", bufs=4))
-        ftp = ctx.enter_context(tc.tile_pool(name="ftp", bufs=2))
+        ftp = ctx.enter_context(tc.tile_pool(name="ftp", bufs=3))
         fgp = ctx.enter_context(tc.tile_pool(name="fgp", bufs=3))
         psum = ctx.enter_context(tc.psum_pool(name="psum", bufs=1))
-        if MANUAL:
-            ctx.enter_context(tc.manual_schedule())
+        ctx.enter_context(tc.manual_schedule())
 
         dummy = keep.tile([P, 1], F32, name="dummy")
         nc.vector.memset(dummy[:], 0.0)
@@ -46,65 +43,81 @@ def tile_coarsematching_w_kernel(tc, feat_c0, feat_c1, W_words, W_scales, b, h0c
         nc.scalar.activation(out=dummy2[:], in_=dummy[:], func=ACT.Exp)
         brow = keep.tile([P, P], BF16, name="brow")
         nc.vector.memset(brow[:], 0.0)
+        nc.scalar.dma_start(out=brow[0 : C // P, :], in_=b.rearrange("(j p) -> j p", p=P))
         planes = keep.tile([P, 2, C], U8, name="planes", align_bytes=64)
         for a in range(2):
             nc.vector.memset(planes[:, a, :].bitcast(I32), 0)
         ident = keep.tile([P, P], F32, name="ident")
         make_identity(nc, ident[:])
 
-        xraw = []
-        for h in range(2):
-            pair = []
+        xraw = {}
+        wt = {}
+
+        def load_x(h):
             for s in range(2):
-                xr = keep.tile([P, C // 2], BF16, name="xraw%d_%d" % (h, s))
-                nc.sync.dma_start(out=xr[:], in_=feats[s][:, (C // 2) * h : (C // 2) * (h + 1)])
-                pair.append(xr)
-            xraw.append(pair)
-        nc.scalar.dma_start(out=brow[0 : C // P, :], in_=b.rearrange("(j p) -> j p", p=P))
-        for a in range(2):
+                xr = keep.tile([P, half], BF16, name="xraw%d_%d" % (h, s))
+                nc.sync.dma_start(out=xr[:], in_=feats[s][:, half * h : half * (h + 1)])
+                xraw[(h, s)] = xr
+
+        def load_scales(a):
             for q in range(4):
                 nc.sync.dma_start(
                     out=planes[32 * q : 32 * q + 16, a, :].bitcast(I32),
                     in_=W_scales[4 * a : 4 * a + 4, 4 * q : 4 * q + 4, :].bitcast(I32),
                 )
-        wt = []
-        for c in range(NCHUNK):
-            row = []
+
+        def load_w(c, g):
+            first, count = CHUNKS[c]
+            w = keep.tile([P, P * count], U32, name="w%d_%d" % (c, g), align_bytes=64)
+            nc.sync.dma_start(
+                out=w[:].bitcast(I32),
+                in_=W_words[g].rearrange("p n t -> p (n t)")[:, 4 * P * first : 4 * P * (first + count)].bitcast(I32),
+            )
+            wt[(c, g)] = w
+
+        for a in range(2):
+            load_x(a)
+            load_scales(a)
+            for g in range(4 * a, 4 * a + 4):
+                load_w(0, g)
+        for c in range(1, len(CHUNKS)):
             for g in range(GROUPS):
-                w = keep.tile([P, CHUNK], U32, name="w%d_%d" % (c, g), align_bytes=64)
-                nc.sync.dma_start(
-                    out=w[:].bitcast(I32),
-                    in_=W_words[g].rearrange("p n t -> p (n t)")[:, 4 * CHUNK * c : 4 * CHUNK * (c + 1)].bitcast(I32),
-                )
-                row.append(w)
-            wt.append(row)
+                load_w(c, g)
 
         rows = []
-        for i, (h, w) in enumerate(((h0c, w0c), (h1c, w1c))):
+        for i, (gh, gw) in enumerate(((h0c, w0c), (h1c, w1c))):
             r = keep.tile([P, P], F32, name="rowmask%d" % i)
             nc.vector.memset(r[:], 0.0)
-            nc.vector.memset(r[:].rearrange("p (r c) -> p r c", c=w)[:, BORDER : h - BORDER, BORDER : w - BORDER], 1.0)
+            nc.vector.memset(
+                r[:].rearrange("p (r c) -> p r c", c=gw)[:, BORDER : gh - BORDER, BORDER : gw - BORDER], 1.0
+            )
             rows.append(r)
-        setup_ps = psum.tile([P, 2, P], F32, tag="bank7", name="setup_ps")
+        setup_ps = psum.tile([P, 3, P], F32, tag="bank0", name="setup_ps")
         for i in range(2):
             nc.tensor.transpose(setup_ps[:, i, :], rows[i][:], ident[:])
         im = keep.tile([P, P], F32, name="im")
         nc.vector.tensor_tensor(out=im[:], in0=setup_ps[:, 0, :], in1=rows[1][:], op=ALU.mult)
         imt = keep.tile([P, P], F32, name="imt")
         nc.vector.tensor_tensor(out=imt[:], in0=setup_ps[:, 1, :], in1=rows[0][:], op=ALU.mult)
+        bq = keep.tile([P, P], F32, name="bq")
+        nc.vector.tensor_scalar_mul(bq[:], brow[:], 1.0 / 64.0)
+        bias_t = keep.tile([P, C // P], F32, name="bias_t")
 
         xcodes = keep.tile([P, GROUPS, TOK], U32, name="xcodes", align_bytes=64)
         xplanes = keep.tile([P, GROUPS, TOK], U8, name="xplanes", align_bytes=64)
-        xts = []
-        for g in range(GROUPS):
-            xt = psum.tile([P, 2, TOK], F32, tag="bank%d" % g, name="xt%d" % g)
-            for s in range(2):
-                words = xraw[g // 4][s][:].bitcast(F32)
-                for u in range(2):
-                    lo = 256 * (g % 4)
-                    nc.tensor.transpose(xt[:, u, P * s : P * (s + 1)], words[:, lo + u : lo + 256 : 2], ident[:])
-            xts.append(xt)
+        xts = {}
         xgs = {}
+
+        def x_transposes(h, s):
+            words = xraw[(h, s)][:].bitcast(F32)
+            for gl in range(4):
+                g = 4 * h + gl
+                if s == 0:
+                    xts[g] = psum.tile([P, 2, TOK], F32, tag="bank%d" % (4 + gl), name="xt%d" % g)
+                for u in range(2):
+                    nc.tensor.transpose(
+                        xts[g][:, u, P * s : P * (s + 1)], words[:, 256 * gl + u : 256 * (gl + 1) : 2], ident[:]
+                    )
 
         def x_copy(g):
             xg = xgp.tile([P, 4 * TOK], BF16, name="xg", align_bytes=64)
@@ -119,70 +132,81 @@ def tile_coarsematching_w_kernel(tc, feat_c0, feat_c1, W_words, W_scales, b, h0c
         def x_quant(g):
             nc.vector.quantize_mx(out=xcodes[:, g, :].bitcast(FP8X4), scales=xplanes[:, g, :], in_=xgs[g][:])
 
-        x_copy(0)
-        x_copy(1)
-        for g in range(GROUPS):
-            if g + 2 < GROUPS:
-                x_copy(g + 2)
-            x_quant(g)
-
-        bq = keep.tile([P, P], F32, name="bq")
-        nc.vector.tensor_scalar_mul(bq[:], brow[:], 1.0 / 64.0)
-        bias_ps = psum.tile([P, P], F32, tag="bank0", name="bias_ps")
-        nc.tensor.transpose(bias_ps[:], bq[:], ident[:])
-        bias_t = keep.tile([P, C // P], F32, name="bias_t")
-        nc.vector.tensor_copy(out=bias_t[:], in_=bias_ps[:, 0 : C // P])
+        def x_finish(h):
+            for gl in range(4):
+                x_copy(4 * h + gl)
+            for gl in range(4):
+                x_quant(4 * h + gl)
 
         fcodes = keep.tile([P, GROUPS, TOK], U32, name="fcodes", align_bytes=64)
         fplanes = keep.tile([P, GROUPS, TOK], U8, name="fplanes", align_bytes=64)
-        for c in range(NCHUNK):
-            accs = []
-            for j in range(TILES):
-                acc = psum.tile([P, TOK], F32, tag="bank%d" % j, name="acc%d_%d" % (c, j))
-                accs.append(acc)
-            for g in range(GROUPS):
+        accs = {}
+
+        def stage1(c, g_lo, g_hi):
+            first, count = CHUNKS[c]
+            for g in range(g_lo, g_hi):
                 k = 4 * (g % 4)
-                for j in range(TILES):
+                for j in range(count):
+                    n = first + j
+                    if g == 0:
+                        accs[n] = psum.tile([P, TOK], F32, tag="bank%d" % (n % BANKS), name="acc%d" % n)
                     nc.tensor.matmul_mx(
-                        out=accs[j][:],
-                        lhsT=wt[c][g][:, P * j : P * (j + 1)].bitcast(FP8X4),
-                        lhsT_scale=planes[k:P, g // 4, CHUNK * c + P * j : CHUNK * c + P * (j + 1)],
+                        out=accs[n][:],
+                        lhsT=wt[(c, g)][:, P * j : P * (j + 1)].bitcast(FP8X4),
+                        lhsT_scale=planes[k:P, g // 4, P * n : P * (n + 1)],
                         rhs=xcodes[:, g, :].bitcast(FP8X4),
                         rhs_scale=xplanes[:, g, :],
                         start=(g == 0),
                         stop=(g == GROUPS - 1),
                     )
-            ft = ftp.tile([P, TILES, TOK], BF16, name="ft")
-            for j in range(TILES):
-                col = TILES * c + j
+
+        def finish(c):
+            first, count = CHUNKS[c]
+            fts = {}
+            for j in range(count):
+                n = first + j
+                if n % 4 == 0:
+                    fts[n // 4] = ftp.tile([P, 4, TOK], BF16, name="ft")
+                dst = fts[n // 4][:, n % 4, :]
                 if j % 2 == 0:
                     nc.scalar.activation(
-                        out=ft[:, j, :], in_=accs[j][:], func=ACT.Identity, bias=bias_t[:, col : col + 1], scale=1.0 / 64.0
+                        out=dst, in_=accs[n][:], func=ACT.Identity, bias=bias_t[:, n : n + 1], scale=1.0 / 64.0
                     )
                 else:
                     nc.vector.tensor_scalar(
-                        out=ft[:, j, :], in0=accs[j][:], scalar1=1.0 / 64.0, scalar2=bias_t[:, col : col + 1],
+                        out=dst, in0=accs[n][:], scalar1=1.0 / 64.0, scalar2=bias_t[:, n : n + 1],
                         op0=ALU.mult, op1=ALU.add,
                     )
-            fgs = []
-            for h in range(2):
+            fgs = {}
+            for c2 in sorted(fts):
                 fg = fgp.tile([P, 4 * TOK], BF16, name="fg", align_bytes=64)
                 nc.vector.tensor_copy(
                     out=fg[:].rearrange("p (c i t) -> p c t i", i=4, t=4),
-                    in_=ft[:, 4 * h : 4 * h + 4, :].rearrange("p t (c i) -> p c t i", i=4),
+                    in_=fts[c2][:].rearrange("p t (c i) -> p c t i", i=4),
                 )
-                fgs.append(fg)
-            for h in range(2):
-                nc.vector.quantize_mx(
-                    out=fcodes[:, 2 * c + h, :].bitcast(FP8X4), scales=fplanes[:, 2 * c + h, :], in_=fgs[h][:]
-                )
+                fgs[c2] = fg
+            for c2 in sorted(fts):
+                nc.vector.quantize_mx(out=fcodes[:, c2, :].bitcast(FP8X4), scales=fplanes[:, c2, :], in_=fgs[c2][:])
+
+        x_transposes(0, 0)
+        nc.tensor.transpose(setup_ps[:, 2, :], bq[:], ident[:])
+        nc.vector.tensor_copy(out=bias_t[:], in_=setup_ps[:, 2, 0 : C // P])
+        x_transposes(0, 1)
+        x_finish(0)
+        stage1(0, 0, 4)
+        x_transposes(1, 0)
+        x_transposes(1, 1)
+        x_finish(1)
+        stage1(0, 4, GROUPS)
+        finish(0)
+        for c in range(1, len(CHUNKS)):
+            stage1(c, 0, GROUPS)
+            finish(c)
 
         sim_t = psum.tile([P, P], F32, tag="bank0", name="sim_t")
         sim = psum.tile([P, P], F32, tag="bank1", name="sim")
-        sim_t2 = psum.tile([P, P], F32, tag="bank2", name="sim_t2")
-        sim2 = psum.tile([P, P], F32, tag="bank3", name="sim2")
         for c2 in range(GROUPS):
-            for dst, lo_l, lo_r in ((sim_t, P, 0), (sim, 0, P), (sim_t2, P, 0), (sim2, 0, P)):
+            for dst, lo_l, lo_r in ((sim_t, P, 0), (sim, 0, P)):
                 nc.tensor.matmul_mx(
                     out=dst[:],
                     lhsT=fcodes[:, c2, lo_l : lo_l + P].bitcast(FP8X4),
@@ -193,31 +217,36 @@ def tile_coarsematching_w_kernel(tc, feat_c0, feat_c1, W_words, W_scales, b, h0c
                     stop=(c2 == GROUPS - 1),
                 )
 
-        mx = keep.tile([P, 2], F32, name="mx")
         nb = keep.tile([P, 2], F32, name="nb")
         sums = keep.tile([P, 2], F32, name="sums")
         rec = keep.tile([P, 2], F32, name="rec")
-        e_t = keep.tile([P, P], F32, name="e_t")
-        e_n = keep.tile([P, P], F32, name="e_n")
+        neg = []
         for i, ps in enumerate((sim_t, sim)):
-            nc.vector.reduce_max(out=mx[:, i : i + 1], in_=ps[:], axis=AX.X)
-            nc.vector.tensor_scalar_mul(nb[:, i : i + 1], mx[:, i : i + 1], -INV_T)
-        for i, (ps, e) in enumerate(((sim_t, e_t), (sim, e_n))):
-            nc.scalar.activation(
-                out=e[:], in_=ps[:], func=ACT.Exp, bias=nb[:, i : i + 1], scale=INV_T, accum_out=sums[:, i : i + 1]
+            ng = keep.tile([P, P], F32, name="neg%d" % i)
+            nc.vector.tensor_scalar(
+                out=ng[:], in0=ps[:], scalar1=-INV_T, scalar2=None, op0=ALU.mult, op1=ALU.min,
+                accum_out=nb[:, i : i + 1],
             )
+            neg.append(ng)
+        es = []
+        for i in range(2):
+            e = keep.tile([P, P], F32, name="e%d" % i)
+            nc.scalar.activation(
+                out=e[:], in_=neg[i][:], func=ACT.Exp, bias=nb[:, i : i + 1], scale=-1.0, accum_out=sums[:, i : i + 1]
+            )
+            es.append(e)
         g_t = keep.tile([P, P], F32, name="g_t")
         nc.vector.scalar_tensor_tensor(
-            out=g_t[:], in0=sim_t2[:], scalar=mx[:, 0:1], in1=imt[:], op0=ALU.is_equal, op1=ALU.mult
+            out=g_t[:], in0=neg[0][:], scalar=nb[:, 0:1], in1=imt[:], op0=ALU.is_equal, op1=ALU.mult
         )
         nc.vector.reciprocal(out=rec[:, 0:1], in_=sums[:, 0:1])
         c_t = keep.tile([P, P], F32, name="c_t")
-        nc.vector.tensor_scalar_mul(c_t[:], e_t[:], rec[:, 0:1])
+        nc.vector.tensor_scalar_mul(c_t[:], es[0][:], rec[:, 0:1])
         k_t = keep.tile([P, P], F32, name="k_t")
         nc.vector.scalar_tensor_tensor(out=k_t[:], in0=c_t[:], scalar=THR, in1=g_t[:], op0=ALU.is_gt, op1=ALU.mult)
-        back1 = psum.tile([P, P], F32, tag="bank4", name="back1")
+        back1 = psum.tile([P, P], F32, tag="bank2", name="back1")
         nc.tensor.transpose(back1[:], c_t[:], ident[:])
-        back2 = psum.tile([P, 2, P], F32, tag="bank5", name="back2")
+        back2 = psum.tile([P, 2, P], F32, tag="bank3", name="back2")
         nc.tensor.transpose(back2[:, 0, :], c_t[:], ident[:])
         nc.tensor.transpose(back2[:, 1, :], k_t[:], ident[:])
         c10 = keep.tile([P, P], F32, name="c10")
@@ -226,11 +255,11 @@ def tile_coarsematching_w_kernel(tc, feat_c0, feat_c1, W_words, W_scales, b, h0c
 
         g_n = keep.tile([P, P], F32, name="g_n")
         nc.vector.scalar_tensor_tensor(
-            out=g_n[:], in0=sim2[:], scalar=mx[:, 1:2], in1=im[:], op0=ALU.is_equal, op1=ALU.mult
+            out=g_n[:], in0=neg[1][:], scalar=nb[:, 1:2], in1=im[:], op0=ALU.is_equal, op1=ALU.mult
         )
         nc.vector.reciprocal(out=rec[:, 1:2], in_=sums[:, 1:2])
         own = keep.tile([P, 2, P], F32, name="own")
-        nc.vector.tensor_scalar_mul(own[:, 0, :], e_n[:], rec[:, 1:2])
+        nc.vector.tensor_scalar_mul(own[:, 0, :], es[1][:], rec[:, 1:2])
         nc.sync.dma_start(out=out[0, 0], in_=own[:, 0, :])
         nc.vector.scalar_tensor_tensor(
             out=own[:, 1, :], in0=own[:, 0, :], scalar=THR, in1=g_n[:], op0=ALU.is_gt, op1=ALU.mult

@@ -21,6 +21,7 @@ CHUNKS = ((0, 4), (4, 8), (12, 8), (20, 8), (28, 4))
 THR = 0.2
 INV_T = 10.0
 BORDER = 2
+EARLY = 1536
 
 FLOPS = 2 * TOK * C * C + 2 * P * P * C
 
@@ -49,6 +50,12 @@ def tile_coarsematching_w_kernel(tc, feat_c0, feat_c1, W_words, W_scales, b, h0c
             nc.vector.memset(planes[:, a, :].bitcast(I32), 0)
         ident = keep.tile([P, P], F32, name="ident")
         make_identity(nc, ident[:])
+        for r in range(4):
+            for q in (0, 2, 1, 3):
+                nc.gpsimd.dma_start(
+                    out=planes[32 * q + r : 32 * q + 16 : 4, :, EARLY:C].bitcast(F32),
+                    in_=W_scales[:, 4 * q + r, EARLY:C].rearrange("(a i) n -> i a n", i=4).bitcast(F32),
+                )
 
         xraw = {}
         wt = {}
@@ -62,8 +69,8 @@ def tile_coarsematching_w_kernel(tc, feat_c0, feat_c1, W_words, W_scales, b, h0c
         def load_scales(a):
             for q in range(4):
                 nc.sync.dma_start(
-                    out=planes[32 * q : 32 * q + 16, a, :].bitcast(I32),
-                    in_=W_scales[4 * a : 4 * a + 4, 4 * q : 4 * q + 4, :].bitcast(I32),
+                    out=planes[32 * q : 32 * q + 16, a, 0:EARLY].bitcast(I32),
+                    in_=W_scales[4 * a : 4 * a + 4, 4 * q : 4 * q + 4, 0:EARLY].bitcast(I32),
                 )
 
         def load_w(c, g):

@@ -73,23 +73,30 @@ def tile_coarsematching_w_kernel(tc, feat_c0, feat_c1, W_words, W_scales, b, h0c
                     in_=W_scales[4 * a : 4 * a + 4, 4 * q : 4 * q + 4, 0:EARLY].bitcast(I32),
                 )
 
-        def load_w(c, g):
+        def load_w(c, g, many):
             first, count = CHUNKS[c]
-            w = keep.tile([P, P * count], U32, name="w%d_%d" % (c, g), align_bytes=64)
+            w = keep.tile([P, many, P * count], U32, name="w%d_%d" % (c, g), align_bytes=64)
             nc.sync.dma_start(
                 out=w[:].bitcast(I32),
-                in_=W_words[g].rearrange("p n t -> p (n t)")[:, 4 * P * first : 4 * P * (first + count)].bitcast(I32),
+                in_=W_words[g : g + many]
+                .rearrange("g p n t -> p g (n t)")[:, :, 4 * P * first : 4 * P * (first + count)]
+                .bitcast(I32),
             )
-            wt[(c, g)] = w
+            for i in range(many):
+                wt[(c, g + i)] = w[:, i, :]
 
         for a in range(2):
             load_x(a)
             load_scales(a)
-            for g in range(4 * a, 4 * a + 4):
-                load_w(0, g)
-        for c in range(1, len(CHUNKS)):
-            for g in range(GROUPS):
-                load_w(c, g)
+            for g in range(4 * a, 4 * a + 4, 2):
+                load_w(0, g, 2)
+        for c in range(1, len(CHUNKS) - 1):
+            for g in range(0, GROUPS, 2):
+                load_w(c, g, 2)
+        for g in range(0, GROUPS - 2, 2):
+            load_w(len(CHUNKS) - 1, g, 2)
+        for g in range(GROUPS - 2, GROUPS):
+            load_w(len(CHUNKS) - 1, g, 1)
 
         rows = []
         for i, (gh, gw) in enumerate(((h0c, w0c), (h1c, w1c))):

@@ -17,11 +17,11 @@ C = 4096
 GROUPS = C // 512
 TOK = 2 * P
 BANKS = 8
-CHUNKS = ((0, 4), (4, 8), (12, 8), (20, 8), (28, 4))
+PIECES = ((0, 8, 0, 8), (0, 8, 8, 8), (0, 8, 16, 8), (0, 4, 24, 8), (4, 8, 24, 4), (4, 8, 28, 4))
 THR = 0.2
 INV_T = 10.0
 BORDER = 2
-EARLY = 1536
+EARLY = 1024
 
 FLOPS = 2 * TOK * C * C + 2 * P * P * C
 
@@ -73,30 +73,24 @@ def tile_coarsematching_w_kernel(tc, feat_c0, feat_c1, W_words, W_scales, b, h0c
                     in_=W_scales[4 * a : 4 * a + 4, 4 * q : 4 * q + 4, 0:EARLY].bitcast(I32),
                 )
 
-        def load_w(c, g, many):
-            first, count = CHUNKS[c]
-            w = keep.tile([P, many, P * count], U32, name="w%d_%d" % (c, g), align_bytes=64)
+        def load_w(c, g):
+            first, count = PIECES[c][2:4]
+            w = keep.tile([P, P * count], U32, name="w%d_%d" % (c, g), align_bytes=64)
             nc.sync.dma_start(
                 out=w[:].bitcast(I32),
-                in_=W_words[g : g + many]
-                .rearrange("g p n t -> p g (n t)")[:, :, 4 * P * first : 4 * P * (first + count)]
-                .bitcast(I32),
+                in_=W_words[g].rearrange("p n t -> p (n t)")[:, 4 * P * first : 4 * P * (first + count)].bitcast(I32),
             )
-            for i in range(many):
-                wt[(c, g + i)] = w[:, i, :]
+            wt[(c, g)] = w
 
         for a in range(2):
             load_x(a)
+        for a in range(2):
             load_scales(a)
-            for g in range(4 * a, 4 * a + 4, 2):
-                load_w(0, g, 2)
-        for c in range(1, len(CHUNKS) - 1):
-            for g in range(0, GROUPS, 2):
-                load_w(c, g, 2)
-        for g in range(0, GROUPS - 2, 2):
-            load_w(len(CHUNKS) - 1, g, 2)
-        for g in range(GROUPS - 2, GROUPS):
-            load_w(len(CHUNKS) - 1, g, 1)
+            for g in range(4 * a, 4 * a + 4):
+                load_w(0, g)
+        for c in range(1, len(PIECES)):
+            for g in range(PIECES[c][0], PIECES[c][1]):
+                load_w(c, g)
 
         rows = []
         for i, (gh, gw) in enumerate(((h0c, w0c), (h1c, w1c))):
@@ -106,7 +100,7 @@ def tile_coarsematching_w_kernel(tc, feat_c0, feat_c1, W_words, W_scales, b, h0c
                 r[:].rearrange("p (r c) -> p r c", c=gw)[:, BORDER : gh - BORDER, BORDER : gw - BORDER], 1.0
             )
             rows.append(r)
-        setup_ps = psum.tile([P, 3, P], F32, tag="bank0", name="setup_ps")
+        setup_ps = psum.tile([P, 3, P], F32, tag="bank7", name="setup_ps")
         for i in range(2):
             nc.tensor.transpose(setup_ps[:, i, :], rows[i][:], ident[:])
         im = keep.tile([P, P], F32, name="im")
@@ -127,7 +121,7 @@ def tile_coarsematching_w_kernel(tc, feat_c0, feat_c1, W_words, W_scales, b, h0c
             for gl in range(4):
                 g = 4 * h + gl
                 if s == 0:
-                    xts[g] = psum.tile([P, 2, TOK], F32, tag="bank%d" % (4 + gl), name="xt%d" % g)
+                    xts[g] = psum.tile([P, 2, TOK], F32, tag="bank%d" % g, name="xt%d" % g)
                 for u in range(2):
                     nc.tensor.transpose(
                         xts[g][:, u, P * s : P * (s + 1)], words[:, 256 * gl + u : 256 * (gl + 1) : 2], ident[:]
@@ -156,8 +150,8 @@ def tile_coarsematching_w_kernel(tc, feat_c0, feat_c1, W_words, W_scales, b, h0c
         fplanes = keep.tile([P, GROUPS, TOK], U8, name="fplanes", align_bytes=64)
         accs = {}
 
-        def stage1(c, g_lo, g_hi):
-            first, count = CHUNKS[c]
+        def stage1(c):
+            g_lo, g_hi, first, count = PIECES[c]
             for g in range(g_lo, g_hi):
                 k = 4 * (g % 4)
                 for j in range(count):
@@ -174,8 +168,7 @@ def tile_coarsematching_w_kernel(tc, feat_c0, feat_c1, W_words, W_scales, b, h0c
                         stop=(g == GROUPS - 1),
                     )
 
-        def finish(c):
-            first, count = CHUNKS[c]
+        def finish(first, count):
             fts = {}
             for j in range(count):
                 n = first + j
@@ -207,15 +200,13 @@ def tile_coarsematching_w_kernel(tc, feat_c0, feat_c1, W_words, W_scales, b, h0c
         nc.vector.tensor_copy(out=bias_t[:], in_=setup_ps[:, 2, 0 : C // P])
         x_transposes(0, 1)
         x_finish(0)
-        stage1(0, 0, 4)
         x_transposes(1, 0)
         x_transposes(1, 1)
         x_finish(1)
-        stage1(0, 4, GROUPS)
-        finish(0)
-        for c in range(1, len(CHUNKS)):
-            stage1(c, 0, GROUPS)
-            finish(c)
+        for c in range(len(PIECES)):
+            stage1(c)
+            if PIECES[c][1] == GROUPS:
+                finish(PIECES[c][2], PIECES[c][3])
 
         sim_t = psum.tile([P, P], F32, tag="bank0", name="sim_t")
         sim = psum.tile([P, P], F32, tag="bank1", name="sim")

@@ -21,6 +21,7 @@ PIECES = ((0, 8, 0, 8), (0, 8, 8, 8), (0, 8, 16, 8), (0, 4, 24, 8), (4, 8, 24, 4
 THR = 0.2
 INV_T = 10.0
 BORDER = 2
+PAD = 48
 EARLY = 1024
 
 FLOPS = 2 * TOK * C * C + 2 * P * P * C
@@ -45,7 +46,7 @@ def tile_coarsematching_w_kernel(tc, feat_c0, feat_c1, W_words, W_scales, b, h0c
         brow = keep.tile([P, P], BF16, name="brow")
         nc.vector.memset(brow[:], 0.0)
         nc.scalar.dma_start(out=brow[0 : C // P, :], in_=b.rearrange("(j p) -> j p", p=P))
-        planes = keep.tile([P, 2, C], U8, name="planes", align_bytes=64)
+        planes = keep.tile([P, 2, C], U8, name="planes", align_bytes=256)
         for a in range(2):
             nc.vector.memset(planes[:, a, :].bitcast(I32), 0)
         ident = keep.tile([P, P], F32, name="ident")
@@ -75,9 +76,9 @@ def tile_coarsematching_w_kernel(tc, feat_c0, feat_c1, W_words, W_scales, b, h0c
 
         def load_w(c, g):
             first, count = PIECES[c][2:4]
-            w = keep.tile([P, P * count], U32, name="w%d_%d" % (c, g), align_bytes=64)
+            w = keep.tile([P, PAD + P * count], U32, name="w%d_%d" % (c, g), align_bytes=256)
             nc.sync.dma_start(
-                out=w[:].bitcast(I32),
+                out=w[:, PAD:].bitcast(I32),
                 in_=W_words[g].rearrange("p n t -> p (n t)")[:, 4 * P * first : 4 * P * (first + count)].bitcast(I32),
             )
             wt[(c, g)] = w
@@ -111,8 +112,8 @@ def tile_coarsematching_w_kernel(tc, feat_c0, feat_c1, W_words, W_scales, b, h0c
         nc.vector.tensor_scalar_mul(bq[:], brow[:], 1.0 / 64.0)
         bias_t = keep.tile([P, C // P], F32, name="bias_t")
 
-        xcodes = keep.tile([P, GROUPS, TOK], U32, name="xcodes", align_bytes=64)
-        xplanes = keep.tile([P, GROUPS, TOK], U8, name="xplanes", align_bytes=64)
+        xcodes = keep.tile([P, GROUPS, TOK], U32, name="xcodes", align_bytes=256)
+        xplanes = keep.tile([P, GROUPS, TOK], U8, name="xplanes", align_bytes=256)
         xts = {}
         xgs = {}
 
@@ -160,7 +161,7 @@ def tile_coarsematching_w_kernel(tc, feat_c0, feat_c1, W_words, W_scales, b, h0c
                         accs[n] = psum.tile([P, TOK], F32, tag="bank%d" % (n % BANKS), name="acc%d" % n)
                     nc.tensor.matmul_mx(
                         out=accs[n][:],
-                        lhsT=wt[(c, g)][:, P * j : P * (j + 1)].bitcast(FP8X4),
+                        lhsT=wt[(c, g)][:, PAD + P * j : PAD + P * (j + 1)].bitcast(FP8X4),
                         lhsT_scale=planes[k:P, g // 4, P * n : P * (n + 1)],
                         rhs=xcodes[:, g, :].bitcast(FP8X4),
                         rhs_scale=xplanes[:, g, :],

@@ -93,6 +93,8 @@ def tile_coarsematching_w_kernel(tc, feat_c0, feat_c1, W_words, W_scales, b, h0c
             for g in range(PIECES[c][0], PIECES[c][1]):
                 load_w(c, g)
 
+        identb = keep.tile([P, P], BF16, name="identb")
+        nc.vector.tensor_copy(out=identb[:], in_=ident[:])
         rows = []
         for i, (gh, gw) in enumerate(((h0c, w0c), (h1c, w1c))):
             r = keep.tile([P, P], F32, name="rowmask%d" % i)
@@ -196,6 +198,36 @@ def tile_coarsematching_w_kernel(tc, feat_c0, feat_c1, W_words, W_scales, b, h0c
             for c2 in sorted(fts):
                 nc.vector.quantize_mx(out=fcodes[:, c2, :].bitcast(FP8X4), scales=fplanes[:, c2, :], in_=fgs[c2][:])
 
+        def finish_last(first):
+            n0 = first
+            ft = ftp.tile([P, 4, TOK], BF16, name="ft")
+            for j in range(4):
+                n = n0 + j
+                if j % 2 == 0:
+                    nc.scalar.activation(
+                        out=ft[:, j, :], in_=accs[n][:], func=ACT.Identity, bias=bias_t[:, n : n + 1], scale=1.0 / 64.0
+                    )
+                else:
+                    nc.vector.tensor_scalar(
+                        out=ft[:, j, :], in0=accs[n][:], scalar1=1.0 / 64.0, scalar2=bias_t[:, n : n + 1],
+                        op0=ALU.mult, op1=ALU.add,
+                    )
+            c2 = n0 // 4
+            halves = []
+            for h in range(2):
+                fg = fgp.tile([P, 4 * P], BF16, name="fgh", align_bytes=64)
+                nc.vector.tensor_copy(
+                    out=fg[:].rearrange("p (c i t) -> p c t i", i=4, t=4),
+                    in_=ft[:, :, P * h : P * (h + 1)].rearrange("p t (c i) -> p c t i", i=4),
+                )
+                halves.append(fg)
+            for h in range(2):
+                nc.vector.quantize_mx(
+                    out=fcodes[:, c2, P * h : P * (h + 1)].bitcast(FP8X4),
+                    scales=fplanes[:, c2, P * h : P * (h + 1)],
+                    in_=halves[h][:],
+                )
+
         x_transposes(0, 0)
         nc.tensor.transpose(setup_ps[:, 2, :], bq[:], ident[:])
         nc.vector.tensor_copy(out=bias_t[:], in_=setup_ps[:, 2, 0 : C // P])
@@ -206,7 +238,9 @@ def tile_coarsematching_w_kernel(tc, feat_c0, feat_c1, W_words, W_scales, b, h0c
         x_finish(1)
         for c in range(len(PIECES)):
             stage1(c)
-            if PIECES[c][1] == GROUPS:
+            if c == len(PIECES) - 1:
+                finish_last(PIECES[c][2])
+            elif PIECES[c][1] == GROUPS:
                 finish(PIECES[c][2], PIECES[c][3])
 
         sim_t = psum.tile([P, P], F32, tag="bank0", name="sim_t")
@@ -241,37 +275,40 @@ def tile_coarsematching_w_kernel(tc, feat_c0, feat_c1, W_words, W_scales, b, h0c
                 out=e[:], in_=neg[i][:], func=ACT.Exp, bias=nb[:, i : i + 1], scale=-1.0, accum_out=sums[:, i : i + 1]
             )
             es.append(e)
-        g_t = keep.tile([P, P], F32, name="g_t")
-        nc.vector.scalar_tensor_tensor(
-            out=g_t[:], in0=neg[0][:], scalar=nb[:, 0:1], in1=imt[:], op0=ALU.is_equal, op1=ALU.mult
-        )
-        nc.vector.reciprocal(out=rec[:, 0:1], in_=sums[:, 0:1])
-        c_t = keep.tile([P, P], F32, name="c_t")
-        nc.vector.tensor_scalar_mul(c_t[:], es[0][:], rec[:, 0:1])
-        k_t = keep.tile([P, P], F32, name="k_t")
-        nc.vector.scalar_tensor_tensor(out=k_t[:], in0=c_t[:], scalar=THR, in1=g_t[:], op0=ALU.is_gt, op1=ALU.mult)
+        best = []
+        for i, mask in enumerate((imt, im)):
+            g = keep.tile([P, P], BF16, name="best%d" % i)
+            nc.vector.scalar_tensor_tensor(
+                out=g[:], in0=neg[i][:], scalar=nb[:, i : i + 1], in1=mask[:], op0=ALU.is_equal, op1=ALU.mult
+            )
+            best.append(g)
+        conf = []
+        kept = []
+        for i in range(2):
+            nc.vector.reciprocal(out=rec[:, i : i + 1], in_=sums[:, i : i + 1])
+            c = keep.tile([P, P], F32, name="conf%d" % i)
+            nc.vector.tensor_scalar_mul(c[:], es[i][:], rec[:, i : i + 1])
+            k = keep.tile([P, P], BF16, name="kept%d" % i)
+            nc.vector.tensor_scalar(
+                out=k[:], in0=best[i][:], scalar1=rec[:, i : i + 1], scalar2=THR, op0=ALU.mult, op1=ALU.is_gt
+            )
+            conf.append(c)
+            kept.append(k)
         back1 = psum.tile([P, P], F32, tag="bank2", name="back1")
-        nc.tensor.transpose(back1[:], c_t[:], ident[:])
-        back2 = psum.tile([P, 2, P], F32, tag="bank3", name="back2")
-        nc.tensor.transpose(back2[:, 0, :], c_t[:], ident[:])
-        nc.tensor.transpose(back2[:, 1, :], k_t[:], ident[:])
+        back2 = psum.tile([P, P], F32, tag="bank3", name="back2")
+        for back in (back2, back1):
+            nc.tensor.transpose(back[:], conf[0][:], ident[:])
+        votes = psum.tile([P, P], F32, tag="bank4", name="votes")
+        nc.tensor.matmul(votes[:], kept[0][:], identb[:], start=True, stop=False)
+        nc.tensor.matmul(votes[:], identb[:], kept[1][:], start=False, stop=True)
         c10 = keep.tile([P, P], F32, name="c10")
         nc.scalar.copy(out=c10[:], in_=back1[:])
-        nc.sync.dma_start(out=out[1, 0], in_=c10[:])
-
-        g_n = keep.tile([P, P], F32, name="g_n")
-        nc.vector.scalar_tensor_tensor(
-            out=g_n[:], in0=neg[1][:], scalar=nb[:, 1:2], in1=im[:], op0=ALU.is_equal, op1=ALU.mult
-        )
-        nc.vector.reciprocal(out=rec[:, 1:2], in_=sums[:, 1:2])
-        own = keep.tile([P, 2, P], F32, name="own")
-        nc.vector.tensor_scalar_mul(own[:, 0, :], es[1][:], rec[:, 1:2])
-        nc.sync.dma_start(out=out[0, 0], in_=own[:, 0, :])
-        nc.vector.scalar_tensor_tensor(
-            out=own[:, 1, :], in0=own[:, 0, :], scalar=THR, in1=g_n[:], op0=ALU.is_gt, op1=ALU.mult
-        )
-        both = keep.tile([P, 2, P], F32, name="both")
-        nc.vector.tensor_tensor(out=both[:], in0=own[:], in1=back2[:], op=ALU.max)
+        nc.scalar.dma_start(out=out[1, 0], in_=c10[:])
+        nc.sync.dma_start(out=out[0, 0], in_=conf[1][:])
+        larger = keep.tile([P, P], F32, name="larger")
+        nc.vector.tensor_tensor(out=larger[:], in0=conf[1][:], in1=back2[:], op=ALU.max)
         mconf = keep.tile([P, P], F32, name="mconf")
-        nc.vector.tensor_tensor(out=mconf[:], in0=both[:, 0, :], in1=both[:, 1, :], op=ALU.mult)
+        nc.vector.scalar_tensor_tensor(
+            out=mconf[:], in0=votes[:], scalar=1.0, in1=larger[:], op0=ALU.min, op1=ALU.mult
+        )
         nc.sync.dma_start(out=out[2, 0], in_=mconf[:])

from contextlib import ExitStack

import concourse.mybir as mybir
from concourse.masks import make_identity

F32 = mybir.dt.float32
BF16 = mybir.dt.bfloat16
I32 = mybir.dt.int32
U32 = mybir.dt.uint32
U8 = mybir.dt.uint8
FP8X4 = mybir.dt.float8_e4m3fn_x4
ALU = mybir.AluOpType
ACT = mybir.ActivationFunctionType

P = 128
C = 4096
GROUPS = C // 512
TOK = 2 * P
BANKS = 8
PIECES = ((0, 8, 0, 8), (0, 8, 8, 8), (0, 8, 16, 8), (0, 4, 24, 8), (4, 8, 24, 4), (4, 8, 28, 4))
THR = 0.2
INV_T = 10.0
BORDER = 2
PAD = 48
EARLY = 1024

FLOPS = 2 * TOK * C * C + 2 * P * P * C


def tile_coarsematching_w_kernel(tc, feat_c0, feat_c1, W_words, W_scales, b, h0c, w0c, h1c, w1c, out):
    nc = tc.nc
    feats = (feat_c0[0], feat_c1[0])
    half = C // 2
    with ExitStack() as ctx:
        keep = ctx.enter_context(tc.tile_pool(name="keep", bufs=1))
        xgp = ctx.enter_context(tc.tile_pool(name="xgp", bufs=4))
        ftp = ctx.enter_context(tc.tile_pool(name="ftp", bufs=3))
        fgp = ctx.enter_context(tc.tile_pool(name="fgp", bufs=3))
        psum = ctx.enter_context(tc.psum_pool(name="psum", bufs=1))
        ctx.enter_context(tc.manual_schedule())

        dummy = keep.tile([P, 1], F32, name="dummy")
        nc.vector.memset(dummy[:], 0.0)
        dummy2 = keep.tile([P, 1], F32, name="dummy2")
        nc.scalar.activation(out=dummy2[:], in_=dummy[:], func=ACT.Exp)
        brow = keep.tile([P, P], BF16, name="brow")
        nc.vector.memset(brow[:], 0.0)
        nc.scalar.dma_start(out=brow[0 : C // P, :], in_=b.rearrange("(j p) -> j p", p=P))
        planes = keep.tile([P, 2, C], U8, name="planes", align_bytes=256)
        for a in range(2):
            nc.vector.memset(planes[:, a, :].bitcast(I32), 0)
        ident = keep.tile([P, P], F32, name="ident")
        make_identity(nc, ident[:])
        for r in range(4):
            for q in (0, 2, 1, 3):
                nc.gpsimd.dma_start(
                    out=planes[32 * q + r : 32 * q + 16 : 4, :, EARLY:C].bitcast(F32),
                    in_=W_scales[:, 4 * q + r, EARLY:C].rearrange("(a i) n -> i a n", i=4).bitcast(F32),
                )

        xraw = {}
        wt = {}

        def load_x(h):
            for s in range(2):
                xr = keep.tile([P, half], BF16, name="xraw%d_%d" % (h, s))
                nc.sync.dma_start(out=xr[:], in_=feats[s][:, half * h : half * (h + 1)])
                xraw[(h, s)] = xr

        def load_scales(a):
            for q in range(4):
                nc.sync.dma_start(
                    out=planes[32 * q : 32 * q + 16, a, 0:EARLY].bitcast(I32),
                    in_=W_scales[4 * a : 4 * a + 4, 4 * q : 4 * q + 4, 0:EARLY].bitcast(I32),
                )

        def load_w(c, g):
            first, count = PIECES[c][2:4]
            w = keep.tile([P, PAD + P * count], U32, name="w%d_%d" % (c, g), align_bytes=256)
            nc.sync.dma_start(
                out=w[:, PAD:].bitcast(I32),
                in_=W_words[g].rearrange("p n t -> p (n t)")[:, 4 * P * first : 4 * P * (first + count)].bitcast(I32),
            )
            wt[(c, g)] = w

        for a in range(2):
            load_x(a)
        for a in range(2):
            load_scales(a)
            for g in range(4 * a, 4 * a + 4):
                load_w(0, g)
        for c in range(1, len(PIECES)):
            for g in range(PIECES[c][0], PIECES[c][1]):
                load_w(c, g)

        identb = keep.tile([P, P], BF16, name="identb")
        nc.vector.tensor_copy(out=identb[:], in_=ident[:])
        rows = []
        for i, (gh, gw) in enumerate(((h0c, w0c), (h1c, w1c))):
            r = keep.tile([P, P], F32, name="rowmask%d" % i)
            nc.vector.memset(r[:], 0.0)
            nc.vector.memset(
                r[:].rearrange("p (r c) -> p r c", c=gw)[:, BORDER : gh - BORDER, BORDER : gw - BORDER], 1.0
            )
            rows.append(r)
        setup_ps = psum.tile([P, 3, P], F32, tag="bank7", name="setup_ps")
        for i in range(2):
            nc.tensor.transpose(setup_ps[:, i, :], rows[i][:], ident[:])
        im = keep.tile([P, P], F32, name="im")
        nc.vector.tensor_tensor(out=im[:], in0=setup_ps[:, 0, :], in1=rows[1][:], op=ALU.mult)
        imt = keep.tile([P, P], F32, name="imt")
        nc.vector.tensor_tensor(out=imt[:], in0=setup_ps[:, 1, :], in1=rows[0][:], op=ALU.mult)
        bq = keep.tile([P, P], F32, name="bq")
        nc.vector.tensor_scalar_mul(bq[:], brow[:], 1.0 / 64.0)
        bias_t = keep.tile([P, C // P], F32, name="bias_t")

        xcodes = keep.tile([P, GROUPS, TOK], U32, name="xcodes", align_bytes=256)
        xplanes = keep.tile([P, GROUPS, TOK], U8, name="xplanes", align_bytes=256)
        xts = {}
        xgs = {}

        def x_transposes(h, s):
            words = xraw[(h, s)][:].bitcast(F32)
            for gl in range(4):
                g = 4 * h + gl
                if s == 0:
                    xts[g] = psum.tile([P, 2, TOK], F32, tag="bank%d" % g, name="xt%d" % g)
                for u in range(2):
                    nc.tensor.transpose(
                        xts[g][:, u, P * s : P * (s + 1)], words[:, 256 * gl + u : 256 * (gl + 1) : 2], ident[:]
                    )

        def x_copy(g):
            xg = xgp.tile([P, 4 * TOK], BF16, name="xg", align_bytes=64)
            dst = xg[:].bitcast(F32).rearrange("p (k u) -> p k u", u=2)
            src = xts[g][:].rearrange("p u k -> p k u")
            if g % 2 == 0:
                nc.vector.tensor_copy(out=dst, in_=src)
            else:
                nc.scalar.copy(out=dst, in_=src)
            xgs[g] = xg

        def x_quant(g):
            nc.vector.quantize_mx(out=xcodes[:, g, :].bitcast(FP8X4), scales=xplanes[:, g, :], in_=xgs[g][:])

        def x_finish(h):
            for gl in range(4):
                x_copy(4 * h + gl)
            for gl in range(4):
                x_quant(4 * h + gl)

        fcodes = keep.tile([P, GROUPS, TOK], U32, name="fcodes", align_bytes=64)
        fplanes = keep.tile([P, GROUPS, TOK], U8, name="fplanes", align_bytes=64)
        accs = {}

        def stage1(c):
            g_lo, g_hi, first, count = PIECES[c]
            for g in range(g_lo, g_hi):
                k = 4 * (g % 4)
                for j in range(count):
                    n = first + j
                    if g == 0:
                        accs[n] = psum.tile([P, TOK], F32, tag="bank%d" % (n % BANKS), name="acc%d" % n)
                    nc.tensor.matmul_mx(
                        out=accs[n][:],
                        lhsT=wt[(c, g)][:, PAD + P * j : PAD + P * (j + 1)].bitcast(FP8X4),
                        lhsT_scale=planes[k:P, g // 4, P * n : P * (n + 1)],
                        rhs=xcodes[:, g, :].bitcast(FP8X4),
                        rhs_scale=xplanes[:, g, :],
                        start=(g == 0),
                        stop=(g == GROUPS - 1),
                    )

        def finish(first, count):
            fts = {}
            for j in range(count):
                n = first + j
                if n % 4 == 0:
                    fts[n // 4] = ftp.tile([P, 4, TOK], BF16, name="ft")
                dst = fts[n // 4][:, n % 4, :]
                if j % 2 == 0:
                    nc.scalar.activation(
                        out=dst, in_=accs[n][:], func=ACT.Identity, bias=bias_t[:, n : n + 1], scale=1.0 / 64.0
                    )
                else:
                    nc.vector.tensor_scalar(
                        out=dst, in0=accs[n][:], scalar1=1.0 / 64.0, scalar2=bias_t[:, n : n + 1],
                        op0=ALU.mult, op1=ALU.add,
                    )
            fgs = {}
            for c2 in sorted(fts):
                fg = fgp.tile([P, 4 * TOK], BF16, name="fg", align_bytes=64)
                nc.vector.tensor_copy(
                    out=fg[:].rearrange("p (c i t) -> p c t i", i=4, t=4),
                    in_=fts[c2][:].rearrange("p t (c i) -> p c t i", i=4),
                )
                fgs[c2] = fg
            for c2 in sorted(fts):
                nc.vector.quantize_mx(out=fcodes[:, c2, :].bitcast(FP8X4), scales=fplanes[:, c2, :], in_=fgs[c2][:])

        def finish_last(first):
            n0 = first
            ft = ftp.tile([P, 4, TOK], BF16, name="ft")
            for j in range(4):
                n = n0 + j
                if j % 2 == 0:
                    nc.scalar.activation(
                        out=ft[:, j, :], in_=accs[n][:], func=ACT.Identity, bias=bias_t[:, n : n + 1], scale=1.0 / 64.0
                    )
                else:
                    nc.vector.tensor_scalar(
                        out=ft[:, j, :], in0=accs[n][:], scalar1=1.0 / 64.0, scalar2=bias_t[:, n : n + 1],
                        op0=ALU.mult, op1=ALU.add,
                    )
            c2 = n0 // 4
            halves = []
            for h in range(2):
                fg = fgp.tile([P, 4 * P], BF16, name="fgh", align_bytes=64)
                nc.vector.tensor_copy(
                    out=fg[:].rearrange("p (c i t) -> p c t i", i=4, t=4),
                    in_=ft[:, :, P * h : P * (h + 1)].rearrange("p t (c i) -> p c t i", i=4),
                )
                halves.append(fg)
            for h in range(2):
                nc.vector.quantize_mx(
                    out=fcodes[:, c2, P * h : P * (h + 1)].bitcast(FP8X4),
                    scales=fplanes[:, c2, P * h : P * (h + 1)],
                    in_=halves[h][:],
                )

        x_transposes(0, 0)
        nc.tensor.transpose(setup_ps[:, 2, :], bq[:], ident[:])
        nc.vector.tensor_copy(out=bias_t[:], in_=setup_ps[:, 2, 0 : C // P])
        x_transposes(0, 1)
        x_finish(0)
        x_transposes(1, 0)
        x_transposes(1, 1)
        x_finish(1)
        for c in range(len(PIECES)):
            stage1(c)
            if c == len(PIECES) - 1:
                finish_last(PIECES[c][2])
            elif PIECES[c][1] == GROUPS:
                finish(PIECES[c][2], PIECES[c][3])

        sim_t = psum.tile([P, P], F32, tag="bank0", name="sim_t")
        sim = psum.tile([P, P], F32, tag="bank1", name="sim")
        for c2 in range(GROUPS):
            for dst, lo_l, lo_r in ((sim_t, P, 0), (sim, 0, P)):
                nc.tensor.matmul_mx(
                    out=dst[:],
                    lhsT=fcodes[:, c2, lo_l : lo_l + P].bitcast(FP8X4),
                    lhsT_scale=fplanes[:, c2, lo_l : lo_l + P],
                    rhs=fcodes[:, c2, lo_r : lo_r + P].bitcast(FP8X4),
                    rhs_scale=fplanes[:, c2, lo_r : lo_r + P],
                    start=(c2 == 0),
                    stop=(c2 == GROUPS - 1),
                )

        nb = keep.tile([P, 2], F32, name="nb")
        sums = keep.tile([P, 2], F32, name="sums")
        rec = keep.tile([P, 2], F32, name="rec")
        neg = []
        for i, ps in enumerate((sim_t, sim)):
            ng = keep.tile([P, P], F32, name="neg%d" % i)
            nc.vector.tensor_scalar(
                out=ng[:], in0=ps[:], scalar1=-INV_T, scalar2=None, op0=ALU.mult, op1=ALU.min,
                accum_out=nb[:, i : i + 1],
            )
            neg.append(ng)
        es = []
        for i in range(2):
            e = keep.tile([P, P], F32, name="e%d" % i)
            nc.scalar.activation(
                out=e[:], in_=neg[i][:], func=ACT.Exp, bias=nb[:, i : i + 1], scale=-1.0, accum_out=sums[:, i : i + 1]
            )
            es.append(e)
        best = []
        for i, mask in enumerate((imt, im)):
            g = keep.tile([P, P], BF16, name="best%d" % i)
            nc.vector.scalar_tensor_tensor(
                out=g[:], in0=neg[i][:], scalar=nb[:, i : i + 1], in1=mask[:], op0=ALU.is_equal, op1=ALU.mult
            )
            best.append(g)
        conf = []
        kept = []
        for i in range(2):
            nc.vector.reciprocal(out=rec[:, i : i + 1], in_=sums[:, i : i + 1])
            c = keep.tile([P, P], F32, name="conf%d" % i)
            nc.vector.tensor_scalar_mul(c[:], es[i][:], rec[:, i : i + 1])
            k = keep.tile([P, P], BF16, name="kept%d" % i)
            nc.vector.tensor_scalar(
                out=k[:], in0=best[i][:], scalar1=rec[:, i : i + 1], scalar2=THR, op0=ALU.mult, op1=ALU.is_gt
            )
            conf.append(c)
            kept.append(k)
        back1 = psum.tile([P, P], F32, tag="bank2", name="back1")
        back2 = psum.tile([P, P], F32, tag="bank3", name="back2")
        for back in (back2, back1):
            nc.tensor.transpose(back[:], conf[0][:], ident[:])
        votes = psum.tile([P, P], F32, tag="bank4", name="votes")
        nc.tensor.matmul(votes[:], kept[0][:], identb[:], start=True, stop=False)
        nc.tensor.matmul(votes[:], identb[:], kept[1][:], start=False, stop=True)
        c10 = keep.tile([P, P], F32, name="c10")
        nc.scalar.copy(out=c10[:], in_=back1[:])
        nc.scalar.dma_start(out=out[1, 0], in_=c10[:])
        nc.sync.dma_start(out=out[0, 0], in_=conf[1][:])
        larger = keep.tile([P, P], F32, name="larger")
        nc.vector.tensor_tensor(out=larger[:], in0=conf[1][:], in1=back2[:], op=ALU.max)
        mconf = keep.tile([P, P], F32, name="mconf")
        nc.vector.scalar_tensor_tensor(
            out=mconf[:], in0=votes[:], scalar=1.0, in1=larger[:], op0=ALU.min, op1=ALU.mult
        )
        nc.sync.dma_start(out=out[2, 0], in_=mconf[:])
